import numpy as np
import ml_dtypes


def mxq(x, axis, fmt="e4m3"):
    dtype, down = {"e4m3": (ml_dtypes.float8_e4m3fn, 7), "e5m2": (ml_dtypes.float8_e5m2, 14)}[fmt]
    v = np.moveaxis(np.asarray(x, np.float32).astype(ml_dtypes.bfloat16).astype(np.float64), axis, -1)
    blocks = v.reshape(v.shape[:-1] + (-1, 32))
    amax = np.abs(blocks).max(-1, keepdims=True)
    byte = np.maximum(np.where(amax > 0, np.frexp(amax)[1] - 1 + 127, 0) - down, 1)
    scale = np.exp2(byte - 127.0)
    codes = (blocks / scale).astype(np.float32).astype(dtype).astype(np.float64)
    return np.moveaxis((codes * scale).reshape(v.shape), -1, axis)


WIDE = False


def mx_kscale(k):
    if not WIDE:
        return np.ones(k)
    levels = np.array([10, -10, 5, -5, 0])
    a = np.random.permutation(np.resize(levels, k // 512 * 4)).reshape(k // 512, 4)
    idx = np.arange(k)
    return np.exp2(a[idx // 512, idx % 128 // 32])


BF16 = ml_dtypes.bfloat16


def bf(x):
    return np.asarray(x, np.float32).astype(BF16)


def f64(x):
    return np.asarray(x).astype(np.float64)


B, T, H, DK, DH, E, V = 4, 1024, 8, 64, 64, 1024, 1536
HK = H * DK


def rotate_every_two(u):
    u1 = u[..., ::2]
    u2 = u[..., 1::2]
    return np.stack((-u2, u1), axis=-1).reshape(u.shape)


def theta_shift(u, sin, cos):
    return u * cos + rotate_every_two(u) * sin


def setup_inputs():
    s = mx_kscale(E)
    return {"x": bf(np.random.standard_normal((B, T, E)) * s),
            "sin": bf(np.random.standard_normal((T, DK)) * 0.7),
            "cos": bf(np.random.standard_normal((T, DK)) * 0.7),
            "Wq": bf(np.random.standard_normal((E, HK)) / np.sqrt(E) / s[:, None]),
            "Wk": bf(np.random.standard_normal((E, HK)) / np.sqrt(E) / s[:, None])}


def reference(x, sin, cos, Wq, Wk):
    xq = mxq(f64(x), 2, "e4m3")
    q = (xq @ mxq(f64(Wq), 0, "e4m3")).reshape(B, T, H, DK).transpose(0, 2, 1, 3)
    k = (xq @ mxq(f64(Wk), 0, "e4m3")).reshape(B, T, H, DK).transpose(0, 2, 1, 3)
    qr = theta_shift(q, f64(sin), f64(cos))
    kr = theta_shift(k, f64(sin), f64(cos))
    return qr, kr

@@ -1,0 +1,236 @@
+from contextlib import ExitStack
+
+import concourse.bass as bass
+import concourse.mybir as mybir
+import concourse.tile as tile
+from concourse.masks import make_identity
+
+F32 = mybir.dt.float32
+BF16 = mybir.dt.bfloat16
+U32 = mybir.dt.uint32
+U8 = mybir.dt.uint8
+FP8X4 = mybir.dt.float8_e4m3fn_x4
+MULT = mybir.AluOpType.mult
+ADD = mybir.AluOpType.add
+
+P = 128
+NB, T, E, H, DK = 4, 1024, 1024, 8, 64
+HK = H * DK
+TPP = T // P
+HALF = DK // 2
+NPAIR = NB * TPP // 2
+NUNIT = 2 * NPAIR
+AHEAD = 2
+
+FLOPS = 2 * NB * T * E * 2 * HK
+
+VADD_UNITS = (31,)
+
+
+def tile_multiscaleretention_pa_t_kernel(tc, x, sin, cos, Wq, Wk, out_0, out_1):
+    nc = tc.nc
+    outs = (out_0, out_1)
+    w_dram = (Wq, Wk)
+    with ExitStack() as ctx:
+        const = ctx.enter_context(tc.tile_pool(name="const", bufs=1))
+        xpool = ctx.enter_context(tc.tile_pool(name="xpool", bufs=NB))
+        stage = ctx.enter_context(tc.tile_pool(name="stage", bufs=3))
+        codes = ctx.enter_context(tc.tile_pool(name="codes", bufs=2))
+        prod = ctx.enter_context(tc.tile_pool(name="prod", bufs=3))
+        opool = ctx.enter_context(tc.tile_pool(name="opool", bufs=3))
+        tpsum = ctx.enter_context(tc.psum_pool(name="tpsum", bufs=2))
+        acc = ctx.enter_context(tc.psum_pool(name="acc", bufs=3))
+
+        ident = const.tile([P, P], F32, name="ident")
+        make_identity(nc, ident[:])
+
+        ctx.enter_context(tc.manual_schedule())
+
+        warm_a = const.tile([P, 8], F32, name="warm_a")
+        warm_b = const.tile([P, 8], F32, name="warm_b")
+        nc.vector.memset(warm_a[:], 0.0)
+        nc.scalar.copy(out=warm_b[:], in_=warm_a[:])
+
+        x_sb = [xpool.tile([P, TPP * E], BF16, name="x_sb", tag="x_sb") for b in range(NB)]
+        x_dr = [x[b].rearrange("(p j) k -> p (j k)", j=TPP) for b in range(NB)]
+        w_sb = [const.tile([P, 8, HK], BF16, name="w_sb%d" % qk) for qk in range(2)]
+        w_dr = [w.rearrange("(a p e) c -> p a (e c)", a=4, p=P, e=2) for w in w_dram]
+        cos_sb = const.tile([P, TPP, DK], BF16, name="cos_sb")
+        sin_sb = const.tile([P, TPP, DK], BF16, name="sin_sb")
+
+        def load_w(qk, g):
+            nc.sync.dma_start(
+                out=w_sb[qk][:, 4 * g : 4 * g + 4, :].rearrange("p (a e) c -> p a (e c)", e=2),
+                in_=w_dr[qk][:, 2 * g : 2 * g + 2, :],
+            )
+
+        nc.sync.dma_start(out=x_sb[0][:, 0 : 2 * E], in_=x_dr[0][:, 0 : 2 * E])
+        load_w(0, 0)
+        load_w(0, 1)
+        nc.sync.dma_start(out=cos_sb[:], in_=cos.rearrange("(p j) c -> p j c", j=TPP))
+        nc.sync.dma_start(out=sin_sb[:], in_=sin.rearrange("(p j) c -> p j c", j=TPP))
+        nc.sync.dma_start(out=x_sb[0][:, 2 * E :], in_=x_dr[0][:, 2 * E :])
+        load_w(1, 0)
+        load_w(1, 1)
+        for b in range(1, NB):
+            nc.sync.dma_start(out=x_sb[b][:], in_=x_dr[b])
+
+        tab = const.tile([P, 4, TPP, HALF], F32, name="tab")
+        cos_v = cos_sb[:].rearrange("p t (i j) -> p j t i", j=2)
+        sin_v = sin_sb[:].rearrange("p t (i j) -> p j t i", j=2)
+        nc.gpsimd.tensor_scalar(out=tab[:, 0:2], in0=cos_v, scalar1=1.0, scalar2=0.0, op0=MULT, op1=ADD)
+        nc.gpsimd.tensor_scalar(out=tab[:, 2], in0=sin_v[:, 0], scalar1=-1.0, scalar2=0.0, op0=MULT, op1=ADD)
+        nc.gpsimd.tensor_scalar(out=tab[:, 3], in0=sin_v[:, 1], scalar1=1.0, scalar2=0.0, op0=MULT, op1=ADD)
+
+        w_codes = const.tile([P, 2, 2, HK], U32, name="w_codes", align_bytes=64)
+        w_scales = const.tile([P, 2, 2, HK], U8, name="w_scales", align_bytes=64)
+        w_grp = {}
+
+        def regroup_w(qk, g, j, eng):
+            if (qk, g) not in w_grp:
+                w_grp[(qk, g)] = stage.tile([P, 2, HK // 2, 4], BF16, name="w_grp", tag="w_grp", bufs=4, align_bytes=64)
+            src = w_sb[qk][:, 4 * g : 4 * g + 4, :].rearrange("p t (r j) -> p j r t", j=2)
+            dst = w_grp[(qk, g)]
+            if eng == "v":
+                nc.vector.tensor_copy(out=dst[:, j], in_=src[:, j])
+            else:
+                nc.scalar.copy(out=dst[:, j], in_=src[:, j])
+
+        def quant_w(qk, g):
+            nc.vector.quantize_mx(
+                out=w_codes[:, g, qk, :].bitcast(FP8X4),
+                scales=w_scales[:, g, qk, :],
+                in_=w_grp[(qk, g)][:].rearrange("p j r t -> p (j r t)"),
+            )
+
+        x_grp = {}
+        x_codes = {}
+        x_scales = {}
+
+        def prep(pair):
+            b, pr = divmod(pair, TPP // 2)
+            xf = x_sb[b][:].bitcast(F32)
+            x_grp[pair] = stage.tile([P, 2 * E // 2], F32, name="x_grp", tag="x_grp", align_bytes=64)
+            banks = []
+            for s in range(2):
+                jt = 2 * pr + s
+                tp = tpsum.tile([P, 4, P], F32, name="tp", tag="tp")
+                for w in range(4):
+                    lo = jt * (E // 2) + w * P
+                    nc.tensor.transpose(tp[:, w, :], xf[:, lo : lo + P], ident[:])
+                banks.append(tp)
+            for s in range(2):
+                nc.scalar.copy(
+                    out=x_grp[pair][:, s * (E // 2) : (s + 1) * (E // 2)].rearrange("p (g k u) -> p g k u", g=2, u=2),
+                    in_=banks[s][:].rearrange("p (g u) k -> p g k u", u=2),
+                )
+
+        def quant_x(pair):
+            b, pr = divmod(pair, TPP // 2)
+            if pr == 0:
+                x_codes[b] = codes.tile([P, TPP * 2 * P], U32, name="x_codes", tag="x_codes", align_bytes=64)
+                x_scales[b] = codes.tile([P, TPP * 2 * P], U8, name="x_scales", tag="x_scales", align_bytes=64)
+            lo = pr * 4 * P
+            nc.vector.quantize_mx(
+                out=x_codes[b][:, lo : lo + 4 * P].bitcast(FP8X4),
+                scales=x_scales[b][:, lo : lo + 4 * P],
+                in_=x_grp[pair][:].bitcast(BF16),
+            )
+
+        banks_of = {}
+        o_of = {}
+
+        def unit_key(u):
+            b, r = divmod(u, TPP)
+            qk, pr = divmod(r, TPP // 2)
+            return b, qk, pr
+
+        def matmuls(u):
+            b, qk, pr = unit_key(u)
+            bank_e = acc.tile([P, 512], F32, name="bank_e", tag="bank_e")
+            bank_o = acc.tile([P, 512], F32, name="bank_o", tag="bank_o")
+            banks_of[u] = (bank_e, bank_o)
+            for s in range(2):
+                for j in range(2):
+                    for g in range(2):
+                        lo = (2 * pr + s) * 2 * P + g * P
+                        nc.tensor.matmul_mx(
+                            out=banks_of[u][j][:, 256 * s : 256 * s + 256],
+                            lhsT=x_codes[b][:, lo : lo + P].bitcast(FP8X4),
+                            lhsT_scale=x_scales[b][:, lo : lo + P],
+                            rhs=w_codes[:, g, qk, 256 * j : 256 * j + 256].bitcast(FP8X4),
+                            rhs_scale=w_scales[:, g, qk, 256 * j : 256 * j + 256],
+                            start=(g == 0),
+                            stop=(g == 1),
+                        )
+
+        def table(k, pr):
+            return tab[:, k, 2 * pr : 2 * pr + 2, :].unsqueeze(2).to_broadcast([P, 2, H, HALF])
+
+        def products_and_sum(u):
+            b, qk, pr = unit_key(u)
+            bank_e, bank_o = banks_of[u]
+            ev = bank_e[:].rearrange("p (t h i) -> p t h i", t=2, h=H)
+            ov = bank_o[:].rearrange("p (t h i) -> p t h i", t=2, h=H)
+            t1 = prod.tile([P, 2, H, 2, HALF], F32, name="t1", tag="t1")
+            t2 = prod.tile([P, 2, H, 2, HALF], F32, name="t2", tag="t2")
+            nc.vector.tensor_tensor(out=t1[:, 0].rearrange("p h t i -> p t h i"), in0=ev, in1=table(0, pr), op=MULT)
+            nc.vector.tensor_tensor(out=t2[:, 1].rearrange("p h t i -> p t h i"), in0=ev, in1=table(3, pr), op=MULT)
+            nc.vector.tensor_tensor(out=t1[:, 1].rearrange("p h t i -> p t h i"), in0=ov, in1=table(1, pr), op=MULT)
+            nc.vector.tensor_tensor(out=t2[:, 0].rearrange("p h t i -> p t h i"), in0=ov, in1=table(2, pr), op=MULT)
+            return t1, t2
+
+        def add(u, t1, t2):
+            b, qk, pr = unit_key(u)
+            if pr == 0:
+                o_of[(b, qk)] = opool.tile([P, H, TPP, DK], F32, name="o_sb", tag="o_sb")
+            o_sb = o_of[(b, qk)]
+            eng = nc.vector if u in VADD_UNITS else nc.gpsimd
+            eng.tensor_tensor(
+                out=o_sb[:, :, 2 * pr : 2 * pr + 2, :].rearrange("p h t (i j) -> p h (t i) j", j=2),
+                in0=t1[:].rearrange("p j h t i -> p h (t i) j"),
+                in1=t2[:].rearrange("p j h t i -> p h (t i) j"),
+                op=ADD,
+            )
+            dr = outs[qk][b].rearrange("h (p t) c -> p h t c", t=TPP)
+            if b == NB - 1 and qk == 1:
+                nc.sync.dma_start(out=dr[:, :, 2 * pr : 2 * pr + 2, :], in_=o_sb[:, :, 2 * pr : 2 * pr + 2, :])
+            elif pr == TPP // 2 - 1:
+                nc.sync.dma_start(out=dr, in_=o_sb[:])
+
+        prep(0)
+        regroup_w(0, 0, 0, "v")
+        regroup_w(0, 0, 1, "v")
+        regroup_w(0, 1, 0, "v")
+        regroup_w(0, 1, 1, "s")
+        quant_x(0)
+        quant_w(0, 0)
+        quant_w(0, 1)
+        matmuls(0)
+        for pair in range(1, 4):
+            prep(pair)
+        for g in range(2):
+            for j in range(2):
+                regroup_w(1, g, j, "s")
+
+        prep_at = {}
+        quant_after = {0: [1, 2, 3]}
+        for pair in range(4, NPAIR):
+            bb, pr = divmod(pair, TPP // 2)
+            prep_at[TPP * (bb - 1) + 3 + pr] = pair
+            quant_after[TPP * (bb - 1) + 4 + pr] = [pair]
+
+        issued = 1
+        for u in range(NUNIT):
+            t1, t2 = products_and_sum(u)
+            for pair in quant_after.get(u, []):
+                quant_x(pair)
+            if u == 2:
+                quant_w(1, 0)
+                quant_w(1, 1)
+            while issued < NUNIT and issued <= u + AHEAD:
+                matmuls(issued)
+                issued += 1
+            if u in prep_at:
+                prep(prep_at[u])
+            add(u, t1, t2)

@@ -185,13 +185,22 @@ def tile_multiscaleretention_pa_t_kernel(tc, x, sin, cos, Wq, Wk, out_0, out_1):
             if pr == 0:
                 o_of[(b, qk)] = opool.tile([P, H, TPP, DK], F32, name="o_sb", tag="o_sb")
             o_sb = o_of[(b, qk)]
-            eng = nc.vector if u in VADD_UNITS else nc.gpsimd
-            eng.tensor_tensor(
-                out=o_sb[:, :, 2 * pr : 2 * pr + 2, :].rearrange("p h t (i j) -> p h (t i) j", j=2),
-                in0=t1[:].rearrange("p j h t i -> p h (t i) j"),
-                in1=t2[:].rearrange("p j h t i -> p h (t i) j"),
-                op=ADD,
-            )
+            o_view = o_sb[:, :, 2 * pr : 2 * pr + 2, :].rearrange("p h t (i j) -> p h (t i) j", j=2)
+            if u in VADD_UNITS:
+                nc.vector.tensor_tensor(
+                    out=o_view,
+                    in0=t1[:].rearrange("p j h t i -> p h (t i) j"),
+                    in1=t2[:].rearrange("p j h t i -> p h (t i) j"),
+                    op=ADD,
+                )
+            else:
+                nc.gpsimd.tensor_tensor(
+                    out=t1[:].rearrange("p j h t i -> p (j h t i)"),
+                    in0=t1[:].rearrange("p j h t i -> p (j h t i)"),
+                    in1=t2[:].rearrange("p j h t i -> p (j h t i)"),
+                    op=ADD,
+                )
+                nc.scalar.copy(out=o_view, in_=t1[:].rearrange("p j h t i -> p h (t i) j"))
             dr = outs[qk][b].rearrange("h (p t) c -> p h t c", t=TPP)
             if b == NB - 1 and qk == 1:
                 nc.sync.dma_start(out=dr[:, :, 2 * pr : 2 * pr + 2, :], in_=o_sb[:, :, 2 * pr : 2 * pr + 2, :])

@@ -24,7 +24,7 @@ AHEAD = 2
 
 FLOPS = 2 * NB * T * E * 2 * HK
 
-VADD_UNITS = (31,)
+VADD_UNITS = (5, 10, 15, 20, 25, 31)
 
 
 def tile_multiscaleretention_pa_t_kernel(tc, x, sin, cos, Wq, Wk, out_0, out_1):

@@ -24,7 +24,7 @@ AHEAD = 2
 
 FLOPS = 2 * NB * T * E * 2 * HK
 
-VADD_UNITS = (5, 10, 15, 20, 25, 31)
+VADD_UNITS = (31,)
 
 
 def tile_multiscaleretention_pa_t_kernel(tc, x, sin, cos, Wq, Wk, out_0, out_1):
@@ -174,10 +174,10 @@ def tile_multiscaleretention_pa_t_kernel(tc, x, sin, cos, Wq, Wk, out_0, out_1):
             ov = bank_o[:].rearrange("p (t h i) -> p t h i", t=2, h=H)
             t1 = prod.tile([P, 2, H, 2, HALF], F32, name="t1", tag="t1")
             t2 = prod.tile([P, 2, H, 2, HALF], F32, name="t2", tag="t2")
-            nc.vector.tensor_tensor(out=t1[:, 0].rearrange("p h t i -> p t h i"), in0=ev, in1=table(0, pr), op=MULT)
-            nc.vector.tensor_tensor(out=t2[:, 1].rearrange("p h t i -> p t h i"), in0=ev, in1=table(3, pr), op=MULT)
-            nc.vector.tensor_tensor(out=t1[:, 1].rearrange("p h t i -> p t h i"), in0=ov, in1=table(1, pr), op=MULT)
-            nc.vector.tensor_tensor(out=t2[:, 0].rearrange("p h t i -> p t h i"), in0=ov, in1=table(2, pr), op=MULT)
+            nc.vector.tensor_tensor(out=t1[:, 0].rearrange("p h t i -> p t h i"), in0=table(0, pr), in1=ev, op=MULT)
+            nc.vector.tensor_tensor(out=t2[:, 1].rearrange("p h t i -> p t h i"), in0=table(3, pr), in1=ev, op=MULT)
+            nc.vector.tensor_tensor(out=t1[:, 1].rearrange("p h t i -> p t h i"), in0=table(1, pr), in1=ov, op=MULT)
+            nc.vector.tensor_tensor(out=t2[:, 0].rearrange("p h t i -> p t h i"), in0=table(2, pr), in1=ov, op=MULT)
             return t1, t2
 
         def add(u, t1, t2):

@@ -24,7 +24,7 @@ AHEAD = 2
 
 FLOPS = 2 * NB * T * E * 2 * HK
 
-VADD_UNITS = (31,)
+VADD_BLOCKS = (15,)
 
 
 def tile_multiscaleretention_pa_t_kernel(tc, x, sin, cos, Wq, Wk, out_0, out_1):
@@ -37,7 +37,7 @@ def tile_multiscaleretention_pa_t_kernel(tc, x, sin, cos, Wq, Wk, out_0, out_1):
         stage = ctx.enter_context(tc.tile_pool(name="stage", bufs=3))
         codes = ctx.enter_context(tc.tile_pool(name="codes", bufs=2))
         prod = ctx.enter_context(tc.tile_pool(name="prod", bufs=3))
-        opool = ctx.enter_context(tc.tile_pool(name="opool", bufs=3))
+        opool = ctx.enter_context(tc.tile_pool(name="opool", bufs=4))
         tpsum = ctx.enter_context(tc.psum_pool(name="tpsum", bufs=2))
         acc = ctx.enter_context(tc.psum_pool(name="acc", bufs=3))
 
@@ -138,7 +138,6 @@ def tile_multiscaleretention_pa_t_kernel(tc, x, sin, cos, Wq, Wk, out_0, out_1):
             )
 
         banks_of = {}
-        o_of = {}
 
         def unit_key(u):
             b, r = divmod(u, TPP)
@@ -167,32 +166,43 @@ def tile_multiscaleretention_pa_t_kernel(tc, x, sin, cos, Wq, Wk, out_0, out_1):
         def table(k, pr):
             return tab[:, k, 2 * pr : 2 * pr + 2, :].unsqueeze(2).to_broadcast([P, 2, H, HALF])
 
-        def products_and_sum(u):
+        prod_of = {}
+
+        def products(u):
             b, qk, pr = unit_key(u)
             bank_e, bank_o = banks_of[u]
             ev = bank_e[:].rearrange("p (t h i) -> p t h i", t=2, h=H)
             ov = bank_o[:].rearrange("p (t h i) -> p t h i", t=2, h=H)
-            t1 = prod.tile([P, 2, H, 2, HALF], F32, name="t1", tag="t1")
-            t2 = prod.tile([P, 2, H, 2, HALF], F32, name="t2", tag="t2")
-            nc.vector.tensor_tensor(out=t1[:, 0].rearrange("p h t i -> p t h i"), in0=table(0, pr), in1=ev, op=MULT)
-            nc.vector.tensor_tensor(out=t2[:, 1].rearrange("p h t i -> p t h i"), in0=table(3, pr), in1=ev, op=MULT)
-            nc.vector.tensor_tensor(out=t1[:, 1].rearrange("p h t i -> p t h i"), in0=table(1, pr), in1=ov, op=MULT)
-            nc.vector.tensor_tensor(out=t2[:, 0].rearrange("p h t i -> p t h i"), in0=table(2, pr), in1=ov, op=MULT)
-            return t1, t2
+            if u % 2 == 0:
+                t1 = prod.tile([P, 2, H, 4, HALF], F32, name="t1", tag="t1")
+                t2 = prod.tile([P, 2, H, 4, HALF], F32, name="t2", tag="t2")
+                prod_of[u // 2] = (t1, t2)
+            t1, t2 = prod_of[u // 2]
+            lo = 2 * (u % 2)
 
-        def add(u, t1, t2):
-            b, qk, pr = unit_key(u)
-            if pr == 0:
-                o_of[(b, qk)] = opool.tile([P, H, TPP, DK], F32, name="o_sb", tag="o_sb")
-            o_sb = o_of[(b, qk)]
-            o_view = o_sb[:, :, 2 * pr : 2 * pr + 2, :].rearrange("p h t (i j) -> p h (t i) j", j=2)
-            if u in VADD_UNITS:
-                nc.vector.tensor_tensor(
-                    out=o_view,
-                    in0=t1[:].rearrange("p j h t i -> p h (t i) j"),
-                    in1=t2[:].rearrange("p j h t i -> p h (t i) j"),
-                    op=ADD,
-                )
+            def dst(t, j):
+                return t[:, j, :, lo : lo + 2, :].rearrange("p h t i -> p t h i")
+
+            nc.vector.tensor_tensor(out=dst(t1, 0), in0=ev, in1=table(0, pr), op=MULT)
+            nc.vector.tensor_tensor(out=dst(t2, 1), in0=ev, in1=table(3, pr), op=MULT)
+            nc.vector.tensor_tensor(out=dst(t1, 1), in0=ov, in1=table(1, pr), op=MULT)
+            nc.vector.tensor_tensor(out=dst(t2, 0), in0=ov, in1=table(2, pr), op=MULT)
+
+        def sum_and_store(k):
+            b, qk, pr = unit_key(2 * k)
+            t1, t2 = prod_of[k]
+            o_sb = opool.tile([P, H, 4, DK], F32, name="o_sb", tag="o_sb")
+            dr = outs[qk][b].rearrange("h (p t) c -> p h t c", t=TPP)
+            t0 = 2 * pr
+            if k in VADD_BLOCKS:
+                for lo in (0, 2):
+                    nc.vector.tensor_tensor(
+                        out=o_sb[:, :, lo : lo + 2, :].rearrange("p h t (i j) -> p h (t i) j", j=2),
+                        in0=t1[:, :, :, lo : lo + 2, :].rearrange("p j h t i -> p h (t i) j"),
+                        in1=t2[:, :, :, lo : lo + 2, :].rearrange("p j h t i -> p h (t i) j"),
+                        op=ADD,
+                    )
+                    nc.sync.dma_start(out=dr[:, :, t0 + lo : t0 + lo + 2, :], in_=o_sb[:, :, lo : lo + 2, :])
             else:
                 nc.gpsimd.tensor_tensor(
                     out=t1[:].rearrange("p j h t i -> p (j h t i)"),
@@ -200,12 +210,11 @@ def tile_multiscaleretention_pa_t_kernel(tc, x, sin, cos, Wq, Wk, out_0, out_1):
                     in1=t2[:].rearrange("p j h t i -> p (j h t i)"),
                     op=ADD,
                 )
-                nc.scalar.copy(out=o_view, in_=t1[:].rearrange("p j h t i -> p h (t i) j"))
-            dr = outs[qk][b].rearrange("h (p t) c -> p h t c", t=TPP)
-            if b == NB - 1 and qk == 1:
-                nc.sync.dma_start(out=dr[:, :, 2 * pr : 2 * pr + 2, :], in_=o_sb[:, :, 2 * pr : 2 * pr + 2, :])
-            elif pr == TPP // 2 - 1:
-                nc.sync.dma_start(out=dr, in_=o_sb[:])
+                nc.scalar.copy(
+                    out=o_sb[:].rearrange("p h t (i j) -> p h (t i) j", j=2),
+                    in_=t1[:].rearrange("p j h t i -> p h (t i) j"),
+                )
+                nc.sync.dma_start(out=dr[:, :, t0 : t0 + 4, :], in_=o_sb[:])
 
         prep(0)
         regroup_w(0, 0, 0, "v")
@@ -226,20 +235,21 @@ def tile_multiscaleretention_pa_t_kernel(tc, x, sin, cos, Wq, Wk, out_0, out_1):
         quant_after = {0: [1, 2, 3]}
         for pair in range(4, NPAIR):
             bb, pr = divmod(pair, TPP // 2)
-            prep_at[TPP * (bb - 1) + 3 + pr] = pair
-            quant_after[TPP * (bb - 1) + 4 + pr] = [pair]
+            prep_at[TPP * (bb - 1) + 1 + 2 * pr] = pair
+            quant_after[TPP * (bb - 1) + 3 + 2 * pr] = [pair]
 
         issued = 1
         for u in range(NUNIT):
-            t1, t2 = products_and_sum(u)
-            for pair in quant_after.get(u, []):
-                quant_x(pair)
-            if u == 2:
+            products(u)
+            if u == 3:
                 quant_w(1, 0)
                 quant_w(1, 1)
-            while issued < NUNIT and issued <= u + AHEAD:
+            for pair in quant_after.get(u, []):
+                quant_x(pair)
+            while issued < NUNIT and issued <= u + AHEAD and (issued < 4 or u >= 3):
                 matmuls(issued)
                 issued += 1
             if u in prep_at:
                 prep(prep_at[u])
-            add(u, t1, t2)
+            if u % 2 == 1:
+                sum_and_store(u // 2)

@@ -69,8 +69,8 @@ def tile_multiscaleretention_pa_t_kernel(tc, x, sin, cos, Wq, Wk, out_0, out_1):
         load_w(0, 1)
         nc.sync.dma_start(out=cos_sb[:], in_=cos.rearrange("(p j) c -> p j c", j=TPP))
         nc.sync.dma_start(out=sin_sb[:], in_=sin.rearrange("(p j) c -> p j c", j=TPP))
-        nc.sync.dma_start(out=x_sb[0][:, 2 * E :], in_=x_dr[0][:, 2 * E :])
         load_w(1, 0)
+        nc.sync.dma_start(out=x_sb[0][:, 2 * E :], in_=x_dr[0][:, 2 * E :])
         load_w(1, 1)
         for b in range(1, NB):
             nc.sync.dma_start(out=x_sb[b][:], in_=x_dr[b])
@@ -225,11 +225,12 @@ def tile_multiscaleretention_pa_t_kernel(tc, x, sin, cos, Wq, Wk, out_0, out_1):
         quant_w(0, 0)
         quant_w(0, 1)
         matmuls(0)
+        regroup_w(1, 0, 0, "v")
+        regroup_w(1, 0, 1, "v")
         for pair in range(1, 4):
             prep(pair)
-        for g in range(2):
-            for j in range(2):
-                regroup_w(1, g, j, "s")
+        regroup_w(1, 1, 0, "s")
+        regroup_w(1, 1, 1, "s")
 
         prep_at = {}
         quant_after = {0: [1, 2, 3]}

@@ -236,8 +236,9 @@ def tile_multiscaleretention_pa_t_kernel(tc, x, sin, cos, Wq, Wk, out_0, out_1):
         quant_after = {0: [1, 2, 3]}
         for pair in range(4, NPAIR):
             bb, pr = divmod(pair, TPP // 2)
-            prep_at[TPP * (bb - 1) + 1 + 2 * pr] = pair
-            quant_after[TPP * (bb - 1) + 3 + 2 * pr] = [pair]
+            q_step = TPP * (bb - 1) + 3 + 2 * pr
+            quant_after[q_step] = [pair]
+            prep_at[max(q_step - 4, 1)] = prep_at.get(max(q_step - 4, 1), []) + [pair]
 
         issued = 1
         for u in range(NUNIT):
@@ -250,7 +251,7 @@ def tile_multiscaleretention_pa_t_kernel(tc, x, sin, cos, Wq, Wk, out_0, out_1):
             while issued < NUNIT and issued <= u + AHEAD and (issued < 4 or u >= 3):
                 matmuls(issued)
                 issued += 1
-            if u in prep_at:
-                prep(prep_at[u])
+            for pair in prep_at.get(u, []):
+                prep(pair)
             if u % 2 == 1:
                 sum_and_store(u // 2)

@@ -1,8 +1,6 @@
 from contextlib import ExitStack
 
-import concourse.bass as bass
 import concourse.mybir as mybir
-import concourse.tile as tile
 from concourse.masks import make_identity
 
 F32 = mybir.dt.float32
@@ -14,26 +12,33 @@ MULT = mybir.AluOpType.mult
 ADD = mybir.AluOpType.add
 
 P = 128
-NB, T, E, H, DK = 4, 1024, 1024, 8, 64
-HK = H * DK
-TPP = T // P
-HALF = DK // 2
-NPAIR = NB * TPP // 2
-NUNIT = 2 * NPAIR
+SEQS, TOKENS, E = 4, 1024, 1024
+HEADS, CHANNELS = 8, 64
+COLS = HEADS * CHANNELS
+HALF = CHANNELS // 2
+PLANE = HEADS * HALF
+TOK_PP = TOKENS // P
+WORDS = E // 2
+PASSES = 2
+PACK = 4
+PAIRS_PER_SEQ = TOK_PP // 2
+PAIRS = SEQS * PAIRS_PER_SEQ
+UNITS_PER_SEQ = 2 * PAIRS_PER_SEQ
+UNITS = SEQS * UNITS_PER_SEQ
+BLOCKS = UNITS // 2
+BLOCK_TOK = 4
+Q, K = 0, 1
+FIRST_K_UNIT = PAIRS_PER_SEQ
 AHEAD = 2
 
-FLOPS = 2 * NB * T * E * 2 * HK
-
-VADD_BLOCKS = (15,)
+FLOPS = 2 * SEQS * TOKENS * E * 2 * COLS
 
 
 def tile_multiscaleretention_pa_t_kernel(tc, x, sin, cos, Wq, Wk, out_0, out_1):
     nc = tc.nc
-    outs = (out_0, out_1)
-    w_dram = (Wq, Wk)
     with ExitStack() as ctx:
         const = ctx.enter_context(tc.tile_pool(name="const", bufs=1))
-        xpool = ctx.enter_context(tc.tile_pool(name="xpool", bufs=NB))
+        xpool = ctx.enter_context(tc.tile_pool(name="xpool", bufs=SEQS))
         stage = ctx.enter_context(tc.tile_pool(name="stage", bufs=3))
         codes = ctx.enter_context(tc.tile_pool(name="codes", bufs=2))
         prod = ctx.enter_context(tc.tile_pool(name="prod", bufs=3))
@@ -46,57 +51,63 @@ def tile_multiscaleretention_pa_t_kernel(tc, x, sin, cos, Wq, Wk, out_0, out_1):
 
         ctx.enter_context(tc.manual_schedule())
 
-        warm_a = const.tile([P, 8], F32, name="warm_a")
-        warm_b = const.tile([P, 8], F32, name="warm_b")
-        nc.vector.memset(warm_a[:], 0.0)
-        nc.scalar.copy(out=warm_b[:], in_=warm_a[:])
+        warm_in = const.tile([P, 8], F32, name="warm_in")
+        warm_out = const.tile([P, 8], F32, name="warm_out")
+        nc.vector.memset(warm_in[:], 0.0)
+        nc.scalar.copy(out=warm_out[:], in_=warm_in[:])
 
-        x_sb = [xpool.tile([P, TPP * E], BF16, name="x_sb", tag="x_sb") for b in range(NB)]
-        x_dr = [x[b].rearrange("(p j) k -> p (j k)", j=TPP) for b in range(NB)]
-        w_sb = [const.tile([P, 8, HK], BF16, name="w_sb%d" % qk) for qk in range(2)]
-        w_dr = [w.rearrange("(a p e) c -> p a (e c)", a=4, p=P, e=2) for w in w_dram]
-        cos_sb = const.tile([P, TPP, DK], BF16, name="cos_sb")
-        sin_sb = const.tile([P, TPP, DK], BF16, name="sin_sb")
+        x_sb = [xpool.tile([P, TOK_PP * E], BF16, name="x_sb", tag="x_sb") for b in range(SEQS)]
+        x_dram = [x[b].rearrange("(p j) k -> p (j k)", j=TOK_PP) for b in range(SEQS)]
+        w_sb = [const.tile([P, PASSES * PACK, COLS], BF16, name="w_sb%d" % qk) for qk in (Q, K)]
+        w_dram = [w.rearrange("(a p e) c -> p a (e c)", a=2 * PASSES, p=P, e=2) for w in (Wq, Wk)]
+        cos_sb = const.tile([P, TOK_PP, CHANNELS], BF16, name="cos_sb")
+        sin_sb = const.tile([P, TOK_PP, CHANNELS], BF16, name="sin_sb")
 
         def load_w(qk, g):
             nc.sync.dma_start(
-                out=w_sb[qk][:, 4 * g : 4 * g + 4, :].rearrange("p (a e) c -> p a (e c)", e=2),
-                in_=w_dr[qk][:, 2 * g : 2 * g + 2, :],
+                out=w_sb[qk][:, PACK * g : PACK * (g + 1), :].rearrange("p (a e) c -> p a (e c)", e=2),
+                in_=w_dram[qk][:, 2 * g : 2 * g + 2, :],
             )
 
-        nc.sync.dma_start(out=x_sb[0][:, 0 : 2 * E], in_=x_dr[0][:, 0 : 2 * E])
-        load_w(0, 0)
-        load_w(0, 1)
-        nc.sync.dma_start(out=cos_sb[:], in_=cos.rearrange("(p j) c -> p j c", j=TPP))
-        nc.sync.dma_start(out=sin_sb[:], in_=sin.rearrange("(p j) c -> p j c", j=TPP))
-        load_w(1, 0)
-        nc.sync.dma_start(out=x_sb[0][:, 2 * E :], in_=x_dr[0][:, 2 * E :])
-        load_w(1, 1)
-        for b in range(1, NB):
-            nc.sync.dma_start(out=x_sb[b][:], in_=x_dr[b])
+        first = 2 * E
+        nc.sync.dma_start(out=x_sb[0][:, 0:first], in_=x_dram[0][:, 0:first])
+        load_w(Q, 0)
+        load_w(Q, 1)
+        nc.sync.dma_start(out=cos_sb[:], in_=cos.rearrange("(p j) c -> p j c", j=TOK_PP))
+        nc.sync.dma_start(out=sin_sb[:], in_=sin.rearrange("(p j) c -> p j c", j=TOK_PP))
+        load_w(K, 0)
+        nc.sync.dma_start(out=x_sb[0][:, first:], in_=x_dram[0][:, first:])
+        load_w(K, 1)
+        for b in range(1, SEQS):
+            nc.sync.dma_start(out=x_sb[b][:], in_=x_dram[b])
 
-        tab = const.tile([P, 4, TPP, HALF], F32, name="tab")
-        cos_v = cos_sb[:].rearrange("p t (i j) -> p j t i", j=2)
-        sin_v = sin_sb[:].rearrange("p t (i j) -> p j t i", j=2)
-        nc.gpsimd.tensor_scalar(out=tab[:, 0:2], in0=cos_v, scalar1=1.0, scalar2=0.0, op0=MULT, op1=ADD)
-        nc.gpsimd.tensor_scalar(out=tab[:, 2], in0=sin_v[:, 0], scalar1=-1.0, scalar2=0.0, op0=MULT, op1=ADD)
-        nc.gpsimd.tensor_scalar(out=tab[:, 3], in0=sin_v[:, 1], scalar1=1.0, scalar2=0.0, op0=MULT, op1=ADD)
+        COS_EVEN, COS_ODD, NEG_SIN_EVEN, SIN_ODD = 0, 1, 2, 3
+        tab = const.tile([P, 4, TOK_PP, HALF], F32, name="tab")
+        cos_planes = cos_sb[:].rearrange("p t (i j) -> p j t i", j=2)
+        sin_planes = sin_sb[:].rearrange("p t (i j) -> p j t i", j=2)
+        nc.gpsimd.tensor_scalar(
+            out=tab[:, COS_EVEN : COS_ODD + 1], in0=cos_planes, scalar1=1.0, scalar2=0.0, op0=MULT, op1=ADD
+        )
+        nc.gpsimd.tensor_scalar(
+            out=tab[:, NEG_SIN_EVEN], in0=sin_planes[:, 0], scalar1=-1.0, scalar2=0.0, op0=MULT, op1=ADD
+        )
+        nc.gpsimd.tensor_scalar(
+            out=tab[:, SIN_ODD], in0=sin_planes[:, 1], scalar1=1.0, scalar2=0.0, op0=MULT, op1=ADD
+        )
 
-        w_codes = const.tile([P, 2, 2, HK], U32, name="w_codes", align_bytes=64)
-        w_scales = const.tile([P, 2, 2, HK], U8, name="w_scales", align_bytes=64)
+        w_codes = const.tile([P, PASSES, 2, COLS], U32, name="w_codes", align_bytes=64)
+        w_scales = const.tile([P, PASSES, 2, COLS], U8, name="w_scales", align_bytes=64)
         w_grp = {}
 
-        def regroup_w(qk, g, j, eng):
+        def regroup_w(qk, g, j, copy):
             if (qk, g) not in w_grp:
-                w_grp[(qk, g)] = stage.tile([P, 2, HK // 2, 4], BF16, name="w_grp", tag="w_grp", bufs=4, align_bytes=64)
-            src = w_sb[qk][:, 4 * g : 4 * g + 4, :].rearrange("p t (r j) -> p j r t", j=2)
-            dst = w_grp[(qk, g)]
-            if eng == "v":
-                nc.vector.tensor_copy(out=dst[:, j], in_=src[:, j])
-            else:
-                nc.scalar.copy(out=dst[:, j], in_=src[:, j])
+                w_grp[(qk, g)] = stage.tile(
+                    [P, 2, PLANE, PACK], BF16, name="w_grp", tag="w_grp", bufs=2 * PASSES, align_bytes=64
+                )
+            rows = w_sb[qk][:, PACK * g : PACK * (g + 1), :].rearrange("p t (r j) -> p j r t", j=2)
+            copy(out=w_grp[(qk, g)][:, j], in_=rows[:, j])
 
-        def quant_w(qk, g):
+        def quantise_w(qk, g):
             nc.vector.quantize_mx(
                 out=w_codes[:, g, qk, :].bitcast(FP8X4),
                 scales=w_scales[:, g, qk, :],
@@ -107,151 +118,171 @@ def tile_multiscaleretention_pa_t_kernel(tc, x, sin, cos, Wq, Wk, out_0, out_1):
         x_codes = {}
         x_scales = {}
 
-        def prep(pair):
-            b, pr = divmod(pair, TPP // 2)
-            xf = x_sb[b][:].bitcast(F32)
-            x_grp[pair] = stage.tile([P, 2 * E // 2], F32, name="x_grp", tag="x_grp", align_bytes=64)
+        def transpose_pair(pair):
+            b, r = divmod(pair, PAIRS_PER_SEQ)
+            words = x_sb[b][:].bitcast(F32)
+            x_grp[pair] = stage.tile([P, 2 * WORDS], F32, name="x_grp", tag="x_grp", align_bytes=64)
             banks = []
             for s in range(2):
-                jt = 2 * pr + s
-                tp = tpsum.tile([P, 4, P], F32, name="tp", tag="tp")
-                for w in range(4):
-                    lo = jt * (E // 2) + w * P
-                    nc.tensor.transpose(tp[:, w, :], xf[:, lo : lo + P], ident[:])
-                banks.append(tp)
-            for s in range(2):
-                nc.scalar.copy(
-                    out=x_grp[pair][:, s * (E // 2) : (s + 1) * (E // 2)].rearrange("p (g k u) -> p g k u", g=2, u=2),
-                    in_=banks[s][:].rearrange("p (g u) k -> p g k u", u=2),
-                )
+                bank = tpsum.tile([P, 2 * PASSES, P], F32, name="bank_t", tag="bank_t")
+                for a in range(2 * PASSES):
+                    lo = (2 * r + s) * WORDS + a * P
+                    nc.tensor.transpose(bank[:, a, :], words[:, lo : lo + P], ident[:])
+                banks.append(bank)
+            return banks
 
-        def quant_x(pair):
-            b, pr = divmod(pair, TPP // 2)
-            if pr == 0:
-                x_codes[b] = codes.tile([P, TPP * 2 * P], U32, name="x_codes", tag="x_codes", align_bytes=64)
-                x_scales[b] = codes.tile([P, TPP * 2 * P], U8, name="x_scales", tag="x_scales", align_bytes=64)
-            lo = pr * 4 * P
+        def copy_out(pair, s, bank, copy):
+            copy(
+                out=x_grp[pair][:, s * WORDS : (s + 1) * WORDS].rearrange("p (g k u) -> p g k u", g=PASSES, u=2),
+                in_=bank[:].rearrange("p (g u) k -> p g k u", u=2),
+            )
+
+        def prepare_pair(pair):
+            banks = transpose_pair(pair)
+            for s in range(2):
+                copy_out(pair, s, banks[s], nc.scalar.copy)
+
+        def quantise_x(pair):
+            b, r = divmod(pair, PAIRS_PER_SEQ)
+            if r == 0:
+                x_codes[b] = codes.tile([P, TOK_PP * PASSES * P], U32, name="x_codes", tag="x_codes", align_bytes=64)
+                x_scales[b] = codes.tile([P, TOK_PP * PASSES * P], U8, name="x_scales", tag="x_scales", align_bytes=64)
+            lo = r * 2 * PASSES * P
             nc.vector.quantize_mx(
-                out=x_codes[b][:, lo : lo + 4 * P].bitcast(FP8X4),
-                scales=x_scales[b][:, lo : lo + 4 * P],
+                out=x_codes[b][:, lo : lo + 2 * PASSES * P].bitcast(FP8X4),
+                scales=x_scales[b][:, lo : lo + 2 * PASSES * P],
                 in_=x_grp[pair][:].bitcast(BF16),
             )
 
         banks_of = {}
+        products_of = {}
 
         def unit_key(u):
-            b, r = divmod(u, TPP)
-            qk, pr = divmod(r, TPP // 2)
-            return b, qk, pr
+            b, rest = divmod(u, UNITS_PER_SEQ)
+            qk, r = divmod(rest, PAIRS_PER_SEQ)
+            return b, qk, r
 
         def matmuls(u):
-            b, qk, pr = unit_key(u)
-            bank_e = acc.tile([P, 512], F32, name="bank_e", tag="bank_e")
-            bank_o = acc.tile([P, 512], F32, name="bank_o", tag="bank_o")
+            b, qk, r = unit_key(u)
+            bank_e = acc.tile([P, 2 * PLANE], F32, name="bank_e", tag="bank_e")
+            bank_o = acc.tile([P, 2 * PLANE], F32, name="bank_o", tag="bank_o")
             banks_of[u] = (bank_e, bank_o)
             for s in range(2):
                 for j in range(2):
-                    for g in range(2):
-                        lo = (2 * pr + s) * 2 * P + g * P
+                    for g in range(PASSES):
+                        lo = ((2 * r + s) * PASSES + g) * P
                         nc.tensor.matmul_mx(
-                            out=banks_of[u][j][:, 256 * s : 256 * s + 256],
+                            out=banks_of[u][j][:, PLANE * s : PLANE * (s + 1)],
                             lhsT=x_codes[b][:, lo : lo + P].bitcast(FP8X4),
                             lhsT_scale=x_scales[b][:, lo : lo + P],
-                            rhs=w_codes[:, g, qk, 256 * j : 256 * j + 256].bitcast(FP8X4),
-                            rhs_scale=w_scales[:, g, qk, 256 * j : 256 * j + 256],
+                            rhs=w_codes[:, g, qk, PLANE * j : PLANE * (j + 1)].bitcast(FP8X4),
+                            rhs_scale=w_scales[:, g, qk, PLANE * j : PLANE * (j + 1)],
                             start=(g == 0),
-                            stop=(g == 1),
+                            stop=(g == PASSES - 1),
                         )
 
-        def table(k, pr):
-            return tab[:, k, 2 * pr : 2 * pr + 2, :].unsqueeze(2).to_broadcast([P, 2, H, HALF])
-
-        prod_of = {}
-
         def products(u):
-            b, qk, pr = unit_key(u)
-            bank_e, bank_o = banks_of[u]
-            ev = bank_e[:].rearrange("p (t h i) -> p t h i", t=2, h=H)
-            ov = bank_o[:].rearrange("p (t h i) -> p t h i", t=2, h=H)
+            r = unit_key(u)[2]
             if u % 2 == 0:
-                t1 = prod.tile([P, 2, H, 4, HALF], F32, name="t1", tag="t1")
-                t2 = prod.tile([P, 2, H, 4, HALF], F32, name="t2", tag="t2")
-                prod_of[u // 2] = (t1, t2)
-            t1, t2 = prod_of[u // 2]
+                first_p = prod.tile([P, 2, HEADS, BLOCK_TOK, HALF], F32, name="first_p", tag="first_p")
+                second_p = prod.tile([P, 2, HEADS, BLOCK_TOK, HALF], F32, name="second_p", tag="second_p")
+                products_of[u // 2] = (first_p, second_p)
+            first_p, second_p = products_of[u // 2]
             lo = 2 * (u % 2)
 
-            def dst(t, j):
-                return t[:, j, :, lo : lo + 2, :].rearrange("p h t i -> p t h i")
+            def multiply(dst, j, bank, table):
+                nc.vector.tensor_tensor(
+                    out=dst[:, j, :, lo : lo + 2, :].rearrange("p h t i -> p t h i"),
+                    in0=bank[:].rearrange("p (t h i) -> p t h i", t=2, h=HEADS),
+                    in1=tab[:, table, 2 * r : 2 * r + 2, :].unsqueeze(2).to_broadcast([P, 2, HEADS, HALF]),
+                    op=MULT,
+                )
 
-            nc.vector.tensor_tensor(out=dst(t1, 0), in0=ev, in1=table(0, pr), op=MULT)
-            nc.vector.tensor_tensor(out=dst(t2, 1), in0=ev, in1=table(3, pr), op=MULT)
-            nc.vector.tensor_tensor(out=dst(t1, 1), in0=ov, in1=table(1, pr), op=MULT)
-            nc.vector.tensor_tensor(out=dst(t2, 0), in0=ov, in1=table(2, pr), op=MULT)
+            bank_e, bank_o = banks_of[u]
+            multiply(first_p, 0, bank_e, COS_EVEN)
+            multiply(second_p, 1, bank_e, SIN_ODD)
+            multiply(first_p, 1, bank_o, COS_ODD)
+            multiply(second_p, 0, bank_o, NEG_SIN_EVEN)
 
-        def sum_and_store(k):
-            b, qk, pr = unit_key(2 * k)
-            t1, t2 = prod_of[k]
-            o_sb = opool.tile([P, H, 4, DK], F32, name="o_sb", tag="o_sb")
-            dr = outs[qk][b].rearrange("h (p t) c -> p h t c", t=TPP)
-            t0 = 2 * pr
-            if k in VADD_BLOCKS:
-                for lo in (0, 2):
-                    nc.vector.tensor_tensor(
-                        out=o_sb[:, :, lo : lo + 2, :].rearrange("p h t (i j) -> p h (t i) j", j=2),
-                        in0=t1[:, :, :, lo : lo + 2, :].rearrange("p j h t i -> p h (t i) j"),
-                        in1=t2[:, :, :, lo : lo + 2, :].rearrange("p j h t i -> p h (t i) j"),
-                        op=ADD,
-                    )
-                    nc.sync.dma_start(out=dr[:, :, t0 + lo : t0 + lo + 2, :], in_=o_sb[:, :, lo : lo + 2, :])
-            else:
-                nc.gpsimd.tensor_tensor(
-                    out=t1[:].rearrange("p j h t i -> p (j h t i)"),
-                    in0=t1[:].rearrange("p j h t i -> p (j h t i)"),
-                    in1=t2[:].rearrange("p j h t i -> p (j h t i)"),
+        def out_rows(k):
+            b, qk, r = unit_key(2 * k)
+            rows = (out_0, out_1)[qk][b].rearrange("h (p t) c -> p h t c", t=TOK_PP)
+            return rows[:, :, 2 * r : 2 * r + BLOCK_TOK, :]
+
+        def interleaved(tile_ap):
+            return tile_ap.rearrange("p h t (i j) -> p h (t i) j", j=2)
+
+        def planes(tile_ap):
+            return tile_ap.rearrange("p j h t i -> p h (t i) j")
+
+        def sum_on_gpsimd(k):
+            first_p, second_p = products_of[k]
+            o_sb = opool.tile([P, HEADS, BLOCK_TOK, CHANNELS], F32, name="o_sb", tag="o_sb")
+            nc.gpsimd.tensor_tensor(
+                out=first_p[:].rearrange("p j h t i -> p (j h t i)"),
+                in0=first_p[:].rearrange("p j h t i -> p (j h t i)"),
+                in1=second_p[:].rearrange("p j h t i -> p (j h t i)"),
+                op=ADD,
+            )
+            nc.scalar.copy(out=interleaved(o_sb[:]), in_=planes(first_p[:]))
+            return o_sb
+
+        def sum_on_vector_and_store(k):
+            first_p, second_p = products_of[k]
+            o_sb = opool.tile([P, HEADS, BLOCK_TOK, CHANNELS], F32, name="o_sb", tag="o_sb")
+            for lo in (0, 2):
+                nc.vector.tensor_tensor(
+                    out=interleaved(o_sb[:, :, lo : lo + 2, :]),
+                    in0=planes(first_p[:, :, :, lo : lo + 2, :]),
+                    in1=planes(second_p[:, :, :, lo : lo + 2, :]),
                     op=ADD,
                 )
-                nc.scalar.copy(
-                    out=o_sb[:].rearrange("p h t (i j) -> p h (t i) j", j=2),
-                    in_=t1[:].rearrange("p j h t i -> p h (t i) j"),
-                )
-                nc.sync.dma_start(out=dr[:, :, t0 : t0 + 4, :], in_=o_sb[:])
+                nc.sync.dma_start(out=out_rows(k)[:, :, lo : lo + 2, :], in_=o_sb[:, :, lo : lo + 2, :])
 
-        prep(0)
-        regroup_w(0, 0, 0, "v")
-        regroup_w(0, 0, 1, "v")
-        regroup_w(0, 1, 0, "v")
-        regroup_w(0, 1, 1, "s")
-        quant_x(0)
-        quant_w(0, 0)
-        quant_w(0, 1)
+
+        prepare_pair(0)
+        regroup_w(Q, 0, 0, nc.vector.tensor_copy)
+        regroup_w(Q, 0, 1, nc.vector.tensor_copy)
+        regroup_w(Q, 1, 0, nc.vector.tensor_copy)
+        regroup_w(Q, 1, 1, nc.scalar.copy)
+        quantise_x(0)
+        quantise_w(Q, 0)
+        quantise_w(Q, 1)
         matmuls(0)
-        regroup_w(1, 0, 0, "v")
-        regroup_w(1, 0, 1, "v")
-        for pair in range(1, 4):
-            prep(pair)
-        regroup_w(1, 1, 0, "s")
-        regroup_w(1, 1, 1, "s")
-
-        prep_at = {}
-        quant_after = {0: [1, 2, 3]}
-        for pair in range(4, NPAIR):
-            bb, pr = divmod(pair, TPP // 2)
-            q_step = TPP * (bb - 1) + 3 + 2 * pr
-            quant_after[q_step] = [pair]
-            prep_at[max(q_step - 4, 1)] = prep_at.get(max(q_step - 4, 1), []) + [pair]
+        regroup_w(K, 0, 0, nc.vector.tensor_copy)
+        regroup_w(K, 0, 1, nc.vector.tensor_copy)
 
         issued = 1
-        for u in range(NUNIT):
+        held = None
+        for u in range(UNITS):
             products(u)
-            if u == 3:
-                quant_w(1, 0)
-                quant_w(1, 1)
-            for pair in quant_after.get(u, []):
-                quant_x(pair)
-            while issued < NUNIT and issued <= u + AHEAD and (issued < 4 or u >= 3):
+            k = u // 2
+            if u == 0:
+                for pair in range(1, PAIRS_PER_SEQ):
+                    banks = transpose_pair(pair)
+                    copy_out(pair, 0, banks[0], nc.scalar.copy)
+                    copy_out(pair, 1, banks[1], nc.vector.tensor_copy)
+                    quantise_x(pair)
+                regroup_w(K, 1, 0, nc.scalar.copy)
+                regroup_w(K, 1, 1, nc.scalar.copy)
+            if u == FIRST_K_UNIT - 1:
+                quantise_w(K, 0)
+                quantise_w(K, 1)
+            if u % 2 == 1 and PAIRS_PER_SEQ <= k + 3 < PAIRS:
+                quantise_x(k + 3)
+            while issued < UNITS and issued <= u + AHEAD and (issued < FIRST_K_UNIT or u >= FIRST_K_UNIT - 1):
                 matmuls(issued)
                 issued += 1
-            for pair in prep_at.get(u, []):
-                prep(pair)
+            if u == 1:
+                prepare_pair(PAIRS_PER_SEQ)
+            if u % 2 == 1 and k + 5 < PAIRS:
+                prepare_pair(k + 5)
             if u % 2 == 1:
-                sum_and_store(u // 2)
+                if k < BLOCKS - 2:
+                    o_sb = sum_on_gpsimd(k)
+                    nc.sync.dma_start(out=out_rows(k), in_=o_sb[:])
+                elif k == BLOCKS - 2:
+                    held = sum_on_gpsimd(k)
+                else:
+                    sum_on_vector_and_store(k)
+                    nc.sync.dma_start(out=out_rows(k - 1), in_=held[:])

from contextlib import ExitStack

import concourse.mybir as mybir
from concourse.masks import make_identity

F32 = mybir.dt.float32
BF16 = mybir.dt.bfloat16
U32 = mybir.dt.uint32
U8 = mybir.dt.uint8
FP8X4 = mybir.dt.float8_e4m3fn_x4
MULT = mybir.AluOpType.mult
ADD = mybir.AluOpType.add

P = 128
SEQS, TOKENS, E = 4, 1024, 1024
HEADS, CHANNELS = 8, 64
COLS = HEADS * CHANNELS
HALF = CHANNELS // 2
PLANE = HEADS * HALF
TOK_PP = TOKENS // P
WORDS = E // 2
PASSES = 2
PACK = 4
PAIRS_PER_SEQ = TOK_PP // 2
PAIRS = SEQS * PAIRS_PER_SEQ
UNITS_PER_SEQ = 2 * PAIRS_PER_SEQ
UNITS = SEQS * UNITS_PER_SEQ
BLOCKS = UNITS // 2
BLOCK_TOK = 4
Q, K = 0, 1
FIRST_K_UNIT = PAIRS_PER_SEQ
AHEAD = 2

FLOPS = 2 * SEQS * TOKENS * E * 2 * COLS


def tile_multiscaleretention_pa_t_kernel(tc, x, sin, cos, Wq, Wk, out_0, out_1):
    nc = tc.nc
    with ExitStack() as ctx:
        const = ctx.enter_context(tc.tile_pool(name="const", bufs=1))
        xpool = ctx.enter_context(tc.tile_pool(name="xpool", bufs=SEQS))
        stage = ctx.enter_context(tc.tile_pool(name="stage", bufs=3))
        codes = ctx.enter_context(tc.tile_pool(name="codes", bufs=2))
        prod = ctx.enter_context(tc.tile_pool(name="prod", bufs=3))
        opool = ctx.enter_context(tc.tile_pool(name="opool", bufs=4))
        tpsum = ctx.enter_context(tc.psum_pool(name="tpsum", bufs=2))
        acc = ctx.enter_context(tc.psum_pool(name="acc", bufs=3))

        ident = const.tile([P, P], F32, name="ident")
        make_identity(nc, ident[:])

        ctx.enter_context(tc.manual_schedule())

        warm_in = const.tile([P, 8], F32, name="warm_in")
        warm_out = const.tile([P, 8], F32, name="warm_out")
        nc.vector.memset(warm_in[:], 0.0)
        nc.scalar.copy(out=warm_out[:], in_=warm_in[:])

        x_sb = [xpool.tile([P, TOK_PP * E], BF16, name="x_sb", tag="x_sb") for b in range(SEQS)]
        x_dram = [x[b].rearrange("(p j) k -> p (j k)", j=TOK_PP) for b in range(SEQS)]
        w_sb = [const.tile([P, PASSES * PACK, COLS], BF16, name="w_sb%d" % qk) for qk in (Q, K)]
        w_dram = [w.rearrange("(a p e) c -> p a (e c)", a=2 * PASSES, p=P, e=2) for w in (Wq, Wk)]
        cos_sb = const.tile([P, TOK_PP, CHANNELS], BF16, name="cos_sb")
        sin_sb = const.tile([P, TOK_PP, CHANNELS], BF16, name="sin_sb")

        def load_w(qk, g):
            nc.sync.dma_start(
                out=w_sb[qk][:, PACK * g : PACK * (g + 1), :].rearrange("p (a e) c -> p a (e c)", e=2),
                in_=w_dram[qk][:, 2 * g : 2 * g + 2, :],
            )

        first = 2 * E
        nc.sync.dma_start(out=x_sb[0][:, 0:first], in_=x_dram[0][:, 0:first])
        load_w(Q, 0)
        load_w(Q, 1)
        nc.sync.dma_start(out=cos_sb[:], in_=cos.rearrange("(p j) c -> p j c", j=TOK_PP))
        nc.sync.dma_start(out=sin_sb[:], in_=sin.rearrange("(p j) c -> p j c", j=TOK_PP))
        load_w(K, 0)
        nc.sync.dma_start(out=x_sb[0][:, first:], in_=x_dram[0][:, first:])
        load_w(K, 1)
        for b in range(1, SEQS):
            nc.sync.dma_start(out=x_sb[b][:], in_=x_dram[b])

        COS_EVEN, COS_ODD, NEG_SIN_EVEN, SIN_ODD = 0, 1, 2, 3
        tab = const.tile([P, 4, TOK_PP, HALF], F32, name="tab")
        cos_planes = cos_sb[:].rearrange("p t (i j) -> p j t i", j=2)
        sin_planes = sin_sb[:].rearrange("p t (i j) -> p j t i", j=2)
        nc.gpsimd.tensor_scalar(
            out=tab[:, COS_EVEN : COS_ODD + 1], in0=cos_planes, scalar1=1.0, scalar2=0.0, op0=MULT, op1=ADD
        )
        nc.gpsimd.tensor_scalar(
            out=tab[:, NEG_SIN_EVEN], in0=sin_planes[:, 0], scalar1=-1.0, scalar2=0.0, op0=MULT, op1=ADD
        )
        nc.gpsimd.tensor_scalar(
            out=tab[:, SIN_ODD], in0=sin_planes[:, 1], scalar1=1.0, scalar2=0.0, op0=MULT, op1=ADD
        )

        w_codes = const.tile([P, PASSES, 2, COLS], U32, name="w_codes", align_bytes=64)
        w_scales = const.tile([P, PASSES, 2, COLS], U8, name="w_scales", align_bytes=64)
        w_grp = {}

        def regroup_w(qk, g, j, copy):
            if (qk, g) not in w_grp:
                w_grp[(qk, g)] = stage.tile(
                    [P, 2, PLANE, PACK], BF16, name="w_grp", tag="w_grp", bufs=2 * PASSES, align_bytes=64
                )
            rows = w_sb[qk][:, PACK * g : PACK * (g + 1), :].rearrange("p t (r j) -> p j r t", j=2)
            copy(out=w_grp[(qk, g)][:, j], in_=rows[:, j])

        def quantise_w(qk, g):
            nc.vector.quantize_mx(
                out=w_codes[:, g, qk, :].bitcast(FP8X4),
                scales=w_scales[:, g, qk, :],
                in_=w_grp[(qk, g)][:].rearrange("p j r t -> p (j r t)"),
            )

        x_grp = {}
        x_codes = {}
        x_scales = {}

        def transpose_pair(pair):
            b, r = divmod(pair, PAIRS_PER_SEQ)
            words = x_sb[b][:].bitcast(F32)
            x_grp[pair] = stage.tile([P, 2 * WORDS], F32, name="x_grp", tag="x_grp", align_bytes=64)
            banks = []
            for s in range(2):
                bank = tpsum.tile([P, 2 * PASSES, P], F32, name="bank_t", tag="bank_t")
                for a in range(2 * PASSES):
                    lo = (2 * r + s) * WORDS + a * P
                    nc.tensor.transpose(bank[:, a, :], words[:, lo : lo + P], ident[:])
                banks.append(bank)
            return banks

        def copy_out(pair, s, bank, copy):
            copy(
                out=x_grp[pair][:, s * WORDS : (s + 1) * WORDS].rearrange("p (g k u) -> p g k u", g=PASSES, u=2),
                in_=bank[:].rearrange("p (g u) k -> p g k u", u=2),
            )

        def prepare_pair(pair):
            banks = transpose_pair(pair)
            for s in range(2):
                copy_out(pair, s, banks[s], nc.scalar.copy)

        def quantise_x(pair):
            b, r = divmod(pair, PAIRS_PER_SEQ)
            if r == 0:
                x_codes[b] = codes.tile([P, TOK_PP * PASSES * P], U32, name="x_codes", tag="x_codes", align_bytes=64)
                x_scales[b] = codes.tile([P, TOK_PP * PASSES * P], U8, name="x_scales", tag="x_scales", align_bytes=64)
            lo = r * 2 * PASSES * P
            nc.vector.quantize_mx(
                out=x_codes[b][:, lo : lo + 2 * PASSES * P].bitcast(FP8X4),
                scales=x_scales[b][:, lo : lo + 2 * PASSES * P],
                in_=x_grp[pair][:].bitcast(BF16),
            )

        banks_of = {}
        products_of = {}

        def unit_key(u):
            b, rest = divmod(u, UNITS_PER_SEQ)
            qk, r = divmod(rest, PAIRS_PER_SEQ)
            return b, qk, r

        def matmuls(u):
            b, qk, r = unit_key(u)
            bank_e = acc.tile([P, 2 * PLANE], F32, name="bank_e", tag="bank_e")
            bank_o = acc.tile([P, 2 * PLANE], F32, name="bank_o", tag="bank_o")
            banks_of[u] = (bank_e, bank_o)
            for s in range(2):
                for j in range(2):
                    for g in range(PASSES):
                        lo = ((2 * r + s) * PASSES + g) * P
                        nc.tensor.matmul_mx(
                            out=banks_of[u][j][:, PLANE * s : PLANE * (s + 1)],
                            lhsT=x_codes[b][:, lo : lo + P].bitcast(FP8X4),
                            lhsT_scale=x_scales[b][:, lo : lo + P],
                            rhs=w_codes[:, g, qk, PLANE * j : PLANE * (j + 1)].bitcast(FP8X4),
                            rhs_scale=w_scales[:, g, qk, PLANE * j : PLANE * (j + 1)],
                            start=(g == 0),
                            stop=(g == PASSES - 1),
                        )

        def products(u):
            r = unit_key(u)[2]
            if u % 2 == 0:
                first_p = prod.tile([P, 2, HEADS, BLOCK_TOK, HALF], F32, name="first_p", tag="first_p")
                second_p = prod.tile([P, 2, HEADS, BLOCK_TOK, HALF], F32, name="second_p", tag="second_p")
                products_of[u // 2] = (first_p, second_p)
            first_p, second_p = products_of[u // 2]
            lo = 2 * (u % 2)

            def multiply(dst, j, bank, table):
                nc.vector.tensor_tensor(
                    out=dst[:, j, :, lo : lo + 2, :].rearrange("p h t i -> p t h i"),
                    in0=bank[:].rearrange("p (t h i) -> p t h i", t=2, h=HEADS),
                    in1=tab[:, table, 2 * r : 2 * r + 2, :].unsqueeze(2).to_broadcast([P, 2, HEADS, HALF]),
                    op=MULT,
                )

            bank_e, bank_o = banks_of[u]
            multiply(first_p, 0, bank_e, COS_EVEN)
            multiply(second_p, 1, bank_e, SIN_ODD)
            multiply(first_p, 1, bank_o, COS_ODD)
            multiply(second_p, 0, bank_o, NEG_SIN_EVEN)

        def out_rows(k):
            b, qk, r = unit_key(2 * k)
            rows = (out_0, out_1)[qk][b].rearrange("h (p t) c -> p h t c", t=TOK_PP)
            return rows[:, :, 2 * r : 2 * r + BLOCK_TOK, :]

        def interleaved(tile_ap):
            return tile_ap.rearrange("p h t (i j) -> p h (t i) j", j=2)

        def planes(tile_ap):
            return tile_ap.rearrange("p j h t i -> p h (t i) j")

        def sum_on_gpsimd(k):
            first_p, second_p = products_of[k]
            o_sb = opool.tile([P, HEADS, BLOCK_TOK, CHANNELS], F32, name="o_sb", tag="o_sb")
            nc.gpsimd.tensor_tensor(
                out=first_p[:].rearrange("p j h t i -> p (j h t i)"),
                in0=first_p[:].rearrange("p j h t i -> p (j h t i)"),
                in1=second_p[:].rearrange("p j h t i -> p (j h t i)"),
                op=ADD,
            )
            nc.scalar.copy(out=interleaved(o_sb[:]), in_=planes(first_p[:]))
            return o_sb

        def sum_on_vector_and_store(k):
            first_p, second_p = products_of[k]
            o_sb = opool.tile([P, HEADS, BLOCK_TOK, CHANNELS], F32, name="o_sb", tag="o_sb")
            for lo in (0, 2):
                nc.vector.tensor_tensor(
                    out=interleaved(o_sb[:, :, lo : lo + 2, :]),
                    in0=planes(first_p[:, :, :, lo : lo + 2, :]),
                    in1=planes(second_p[:, :, :, lo : lo + 2, :]),
                    op=ADD,
                )
                nc.sync.dma_start(out=out_rows(k)[:, :, lo : lo + 2, :], in_=o_sb[:, :, lo : lo + 2, :])


        prepare_pair(0)
        regroup_w(Q, 0, 0, nc.vector.tensor_copy)
        regroup_w(Q, 0, 1, nc.vector.tensor_copy)
        regroup_w(Q, 1, 0, nc.vector.tensor_copy)
        regroup_w(Q, 1, 1, nc.scalar.copy)
        quantise_x(0)
        quantise_w(Q, 0)
        quantise_w(Q, 1)
        matmuls(0)
        regroup_w(K, 0, 0, nc.vector.tensor_copy)
        regroup_w(K, 0, 1, nc.vector.tensor_copy)

        issued = 1
        held = None
        for u in range(UNITS):
            products(u)
            k = u // 2
            if u == 0:
                for pair in range(1, PAIRS_PER_SEQ):
                    banks = transpose_pair(pair)
                    copy_out(pair, 0, banks[0], nc.scalar.copy)
                    copy_out(pair, 1, banks[1], nc.vector.tensor_copy)
                    quantise_x(pair)
                regroup_w(K, 1, 0, nc.scalar.copy)
                regroup_w(K, 1, 1, nc.scalar.copy)
            if u == FIRST_K_UNIT - 1:
                quantise_w(K, 0)
                quantise_w(K, 1)
            if u % 2 == 1 and PAIRS_PER_SEQ <= k + 3 < PAIRS:
                quantise_x(k + 3)
            while issued < UNITS and issued <= u + AHEAD and (issued < FIRST_K_UNIT or u >= FIRST_K_UNIT - 1):
                matmuls(issued)
                issued += 1
            if u == 1:
                prepare_pair(PAIRS_PER_SEQ)
            if u % 2 == 1 and k + 5 < PAIRS:
                prepare_pair(k + 5)
            if u % 2 == 1:
                if k < BLOCKS - 2:
                    o_sb = sum_on_gpsimd(k)
                    nc.sync.dma_start(out=out_rows(k), in_=o_sb[:])
                elif k == BLOCKS - 2:
                    held = sum_on_gpsimd(k)
                else:
                    sum_on_vector_and_store(k)
                    nc.sync.dma_start(out=out_rows(k - 1), in_=held[:])
